import numpy as np
import ml_dtypes


BF16 = ml_dtypes.bfloat16


def bf(x):
    return np.asarray(x, np.float32).astype(BF16)


def f64(x):
    return np.asarray(x).astype(np.float64)


E2M1 = np.array([0.0, 0.5, 1.0, 1.5, 2.0, 3.0, 4.0, 6.0, -0.0, -0.5, -1.0, -1.5, -2.0, -3.0, -4.0, -6.0])


def pack_weight(w, fmt):
    k, n = w.shape
    w = f64(bf(w)).reshape(k // 32, 32, n)
    amax = np.abs(w).max(1)
    if fmt == "e4m3":
        byte = np.frexp(amax)[1] - 1 + 127 - 7
    else:
        mant, ex = np.frexp(amax / 6.0)
        byte = np.where(mant > 0.5, ex, ex - 1) + 127
    byte = np.clip(np.where(amax > 0, byte, 1), 1, 254)
    scaled = (w * np.exp2(127.0 - byte)[:, None, :]).reshape(k, n).astype(np.float32)
    by_word = np.ascontiguousarray(scaled.reshape(k // 512, 128, 4, n).transpose(0, 1, 3, 2))
    if fmt == "e4m3":
        words = by_word.astype(ml_dtypes.float8_e4m3fn).view(np.uint8)
    else:
        c = by_word.astype(ml_dtypes.float4_e2m1fn).view(np.uint8) & 0xF
        words = c[..., 0::2] | (c[..., 1::2] << 4)
    return np.ascontiguousarray(words), np.ascontiguousarray(byte.astype(np.uint8).reshape(k // 512, 16, n))


def unpack_weight(words, scales, fmt):
    g, p, n, _ = words.shape
    if fmt == "e4m3":
        vals = np.ascontiguousarray(words).view(ml_dtypes.float8_e4m3fn).astype(np.float64)
    else:
        nib = np.empty((g, p, n, 4), np.uint8)
        nib[..., 0::2] = words & 0xF
        nib[..., 1::2] = words >> 4
        vals = E2M1[nib]
    vals = vals * np.repeat(np.exp2(scales.astype(np.float64) - 127.0), 8, axis=1)[..., None]
    return vals.transpose(0, 1, 3, 2).reshape(g * 512, n)

def pack4(w):
    words, scales = pack_weight(w, "e2m1")
    return words.reshape(words.shape[0], 128, -1), scales


def unpack4(words, scales):
    return unpack_weight(words.reshape(words.shape[0], 128, -1, 2), scales, "e2m1")


def kspread(k):
    return np.exp2(np.repeat(np.random.randint(-6, 7, k // 32), 32).astype(np.float64))


T, D, E = 4096, 4096, 768


def setup_inputs():
    s = kspread(D)
    hidden_states = np.random.standard_normal((T, D)) * s
    hidden_states_words, hidden_states_scales = pack4(np.ascontiguousarray(hidden_states.T))
    weight = np.random.standard_normal((E, D)) * 1.0 / np.sqrt(D) / s[None, :]
    words, scales = pack4(np.ascontiguousarray(weight.T))
    return {"hidden_states_words": hidden_states_words,
            "hidden_states_scales": hidden_states_scales,
            "weight_words": words,
            "weight_scales": scales}


def reference(hidden_states_words, hidden_states_scales, weight_words, weight_scales):
    logits = unpack4(hidden_states_words, hidden_states_scales).T @ unpack4(weight_words, weight_scales)
    return logits

@@ -1,0 +1,117 @@
+from contextlib import ExitStack
+
+import concourse.mybir as mybir
+
+T, D, E = 4096, 4096, 768
+FLOPS = 2 * T * D * E
+
+F32 = mybir.dt.float32
+BF16 = mybir.dt.bfloat16
+I32 = mybir.dt.int32
+U8 = mybir.dt.uint8
+F4 = mybir.dt.float4_e2m1fn_x4
+
+P = 128
+PASSES = D // 512
+CHUNK = 512
+NB = CHUNK // P
+SETS = ((0, 2), (2, 8))
+WARM = 7
+
+
+def tile_longcatrouter_kernel(tc, x_words, x_scales, w_words, w_scales, out):
+    nc = tc.nc
+    with ExitStack() as ctx:
+        keep = ctx.enter_context(tc.tile_pool(name="keep", bufs=1))
+        res = ctx.enter_context(tc.tile_pool(name="res", bufs=6))
+        psum = ctx.enter_context(tc.psum_pool(name="psum", bufs=1))
+        ctx.enter_context(tc.manual_schedule())
+
+        w_codes, w_planes = [], []
+        for i, (a, b) in enumerate(SETS):
+            w_codes.append(keep.tile([P, b - a, 2 * E], U8, align_bytes=256, name="wc%d" % i))
+            w_planes.append(keep.tile([P, b - a, E], U8, align_bytes=256, name="wp%d" % i))
+        x_codes, x_planes = [], []
+        for c in range(T // CHUNK):
+            sets = SETS if c == 0 else ((0, PASSES),)
+            x_codes.append([keep.tile([P, b - a, 2 * CHUNK], U8, align_bytes=256, name="xc%d_%d" % (c, a)) for a, b in sets])
+            x_planes.append([keep.tile([P, b - a, CHUNK], U8, align_bytes=256, name="xp%d_%d" % (c, a)) for a, b in sets])
+
+        def zero(t):
+            nc.vector.memset(t[:].bitcast(I32), 0)
+
+        def load_codes(t, words, a, b, c0, c1):
+            nc.sync.dma_start(out=t[:].bitcast(I32), in_=words[a:b, :, c0:c1].rearrange("g p n -> p g n").bitcast(I32))
+
+        def load_scales(t, scales, a, b, c0, c1):
+            for r in range(4):
+                nc.sync.dma_start(
+                    out=t[r:P:32, :, :].bitcast(I32),
+                    in_=scales[a:b, r:16:4, c0:c1].rearrange("g q n -> q g n").bitcast(I32),
+                )
+
+        warm = keep.tile([P, 512], BF16, name="warm")
+        nc.vector.memset(warm[:], 0.0)
+        for i in range(len(SETS)):
+            zero(w_planes[i])
+            zero(x_planes[0][i])
+        for c in range(1, T // CHUNK):
+            zero(x_planes[c][0])
+
+        for i, (a, b) in enumerate(SETS):
+            load_codes(x_codes[0][i], x_words, a, b, 0, 2 * CHUNK)
+            load_codes(w_codes[i], w_words, a, b, 0, 2 * E)
+            load_scales(w_planes[i], w_scales, a, b, 0, E)
+            load_scales(x_planes[0][i], x_scales, a, b, 0, CHUNK)
+        for c in range(1, T // CHUNK):
+            load_codes(x_codes[c][0], x_words, 0, PASSES, 2 * c * CHUNK, 2 * (c + 1) * CHUNK)
+            load_scales(x_planes[c][0], x_scales, 0, PASSES, c * CHUNK, (c + 1) * CHUNK)
+
+        def bank(k):
+            return psum.tile([P, 512], F32, tag="bank%d" % k, name="bank%d" % k)
+
+        dummy = bank(7)
+        for i in range(WARM):
+            nc.tensor.matmul(dummy[:], warm[:, 0:P], warm[:], start=True, stop=True)
+
+        def mm(acc, c, j, g, n0, n1):
+            ws = 0 if g < SETS[0][1] else 1
+            wg = g - SETS[ws][0]
+            xs, xg = (ws, wg) if c == 0 else (0, g)
+            nc.tensor.matmul_mx(
+                out=acc[:, 0 : n1 - n0],
+                lhsT=x_codes[c][xs][:, xg, 256 * j : 256 * (j + 1)].bitcast(F4),
+                lhsT_scale=x_planes[c][xs][:, xg, P * j : P * (j + 1)],
+                rhs=w_codes[ws][:, wg, 2 * n0 : 2 * n1].bitcast(F4),
+                rhs_scale=w_planes[ws][:, wg, n0:n1],
+                start=(g == 0),
+                stop=(g == PASSES - 1),
+            )
+
+        def finish(big, small, block, last):
+            o = res.tile([P, E], F32, name="o")
+            nc.scalar.copy(out=o[:, 0:512], in_=big[:])
+            nc.vector.tensor_copy(out=o[:, 512:E], in_=small[:, 0:256])
+            rows = out[block * P : (block + 1) * P, :]
+            if last:
+                nc.sync.dma_start(out=rows[:, 0:512], in_=o[:, 0:512])
+                nc.sync.dma_start(out=rows[:, 512:E], in_=o[:, 512:E])
+            else:
+                nc.gpsimd.dma_start(out=rows, in_=o[:])
+
+        accs = [(bank(2 * j), bank(2 * j + 1)) for j in range(NB)]
+        for g in range(PASSES):
+            for j in range(NB):
+                mm(accs[j][0], 0, j, g, 0, 512)
+                mm(accs[j][1], 0, j, g, 512, E)
+        for j in range(NB):
+            finish(accs[j][0], accs[j][1], j, False)
+
+        for block in range(NB, T // P):
+            c, j = block // NB, block % NB
+            big, small = bank(2 * j), bank(2 * j + 1)
+            for g in range(PASSES):
+                mm(big, c, j, g, 0, 512)
+            for g in range(PASSES):
+                mm(small, c, j, g, 512, E)
+            finish(big, small, block, block == T // P - 1)

@@ -15,27 +15,21 @@ P = 128
 PASSES = D // 512
 CHUNK = 512
 NB = CHUNK // P
-SETS = ((0, 2), (2, 8))
-WARM = 7
+NC = T // CHUNK
+WARM = 32
+RUNS = ((0, 3), (3, 8))
 
 
 def tile_longcatrouter_kernel(tc, x_words, x_scales, w_words, w_scales, out):
     nc = tc.nc
     with ExitStack() as ctx:
         keep = ctx.enter_context(tc.tile_pool(name="keep", bufs=1))
-        res = ctx.enter_context(tc.tile_pool(name="res", bufs=6))
+        res = ctx.enter_context(tc.tile_pool(name="res", bufs=8))
         psum = ctx.enter_context(tc.psum_pool(name="psum", bufs=1))
         ctx.enter_context(tc.manual_schedule())
 
-        w_codes, w_planes = [], []
-        for i, (a, b) in enumerate(SETS):
-            w_codes.append(keep.tile([P, b - a, 2 * E], U8, align_bytes=256, name="wc%d" % i))
-            w_planes.append(keep.tile([P, b - a, E], U8, align_bytes=256, name="wp%d" % i))
-        x_codes, x_planes = [], []
-        for c in range(T // CHUNK):
-            sets = SETS if c == 0 else ((0, PASSES),)
-            x_codes.append([keep.tile([P, b - a, 2 * CHUNK], U8, align_bytes=256, name="xc%d_%d" % (c, a)) for a, b in sets])
-            x_planes.append([keep.tile([P, b - a, CHUNK], U8, align_bytes=256, name="xp%d_%d" % (c, a)) for a, b in sets])
+        def alloc(name, passes, width):
+            return keep.tile([P, passes, width], U8, align_bytes=256, name=name)
 
         def zero(t):
             nc.vector.memset(t[:].bitcast(I32), 0)
@@ -50,52 +44,67 @@ def tile_longcatrouter_kernel(tc, x_words, x_scales, w_words, w_scales, out):
                     in_=scales[a:b, r:16:4, c0:c1].rearrange("g q n -> q g n").bitcast(I32),
                 )
 
-        warm = keep.tile([P, 512], BF16, name="warm")
+        warm = keep.tile([P, P], BF16, name="warm")
         nc.vector.memset(warm[:], 0.0)
-        for i in range(len(SETS)):
-            zero(w_planes[i])
-            zero(x_planes[0][i])
-        for c in range(1, T // CHUNK):
-            zero(x_planes[c][0])
 
-        for i, (a, b) in enumerate(SETS):
-            load_codes(x_codes[0][i], x_words, a, b, 0, 2 * CHUNK)
-            load_codes(w_codes[i], w_words, a, b, 0, 2 * E)
-            load_scales(w_planes[i], w_scales, a, b, 0, E)
-            load_scales(x_planes[0][i], x_scales, a, b, 0, CHUNK)
-        for c in range(1, T // CHUNK):
-            load_codes(x_codes[c][0], x_words, 0, PASSES, 2 * c * CHUNK, 2 * (c + 1) * CHUNK)
-            load_scales(x_planes[c][0], x_scales, 0, PASSES, c * CHUNK, (c + 1) * CHUNK)
+        wc = [alloc("wc%d" % g, 1, 2 * E) for g in range(PASSES)]
+        xc0 = [alloc("xc0_%d" % g, 1, 2 * CHUNK) for g in range(PASSES)]
+        wp = [alloc("wp%d" % a, b - a, E) for a, b in RUNS]
+        xp0 = [alloc("xp0_%d" % a, b - a, CHUNK) for a, b in RUNS]
+        xc = [None] + [alloc("xc%d" % c, PASSES, 2 * CHUNK) for c in range(1, NC)]
+        xp = [None] + [alloc("xp%d" % c, PASSES, CHUNK) for c in range(1, NC)]
+        for i in range(len(RUNS)):
+            zero(wp[i])
+            zero(xp0[i])
+        for c in range(1, NC):
+            zero(xp[c])
+
+        for i, (a, b) in enumerate(RUNS):
+            for g in range(a, b):
+                load_codes(xc0[g], x_words, g, g + 1, 0, 2 * CHUNK)
+                load_codes(wc[g], w_words, g, g + 1, 0, 2 * E)
+                if g == a:
+                    load_scales(wp[i], w_scales, a, b, 0, E)
+                    load_scales(xp0[i], x_scales, a, b, 0, CHUNK)
+        for c in range(1, NC):
+            load_codes(xc[c], x_words, 0, PASSES, 2 * c * CHUNK, 2 * (c + 1) * CHUNK)
+            load_scales(xp[c], x_scales, 0, PASSES, c * CHUNK, (c + 1) * CHUNK)
+
+        def run_of(g):
+            for i, (a, b) in enumerate(RUNS):
+                if g < b:
+                    return i, g - a
 
         def bank(k):
             return psum.tile([P, 512], F32, tag="bank%d" % k, name="bank%d" % k)
 
         dummy = bank(7)
         for i in range(WARM):
-            nc.tensor.matmul(dummy[:], warm[:, 0:P], warm[:], start=True, stop=True)
+            nc.tensor.matmul(dummy[:, 0:P], warm[:], warm[:], start=True, stop=True)
 
         def mm(acc, c, j, g, n0, n1):
-            ws = 0 if g < SETS[0][1] else 1
-            wg = g - SETS[ws][0]
-            xs, xg = (ws, wg) if c == 0 else (0, g)
+            i, k = run_of(g)
+            xct, xci, xpt, xpi = (xc0[g], 0, xp0[i], k) if c == 0 else (xc[c], g, xp[c], g)
             nc.tensor.matmul_mx(
                 out=acc[:, 0 : n1 - n0],
-                lhsT=x_codes[c][xs][:, xg, 256 * j : 256 * (j + 1)].bitcast(F4),
-                lhsT_scale=x_planes[c][xs][:, xg, P * j : P * (j + 1)],
-                rhs=w_codes[ws][:, wg, 2 * n0 : 2 * n1].bitcast(F4),
-                rhs_scale=w_planes[ws][:, wg, n0:n1],
+                lhsT=xct[:, xci, 256 * j : 256 * (j + 1)].bitcast(F4),
+                lhsT_scale=xpt[:, xpi, P * j : P * (j + 1)],
+                rhs=wc[g][:, 0, 2 * n0 : 2 * n1].bitcast(F4),
+                rhs_scale=wp[i][:, k, n0:n1],
                 start=(g == 0),
                 stop=(g == PASSES - 1),
             )
 
-        def finish(big, small, block, last):
+        def finish(big, small, block):
             o = res.tile([P, E], F32, name="o")
+            rows = out[block * P : (block + 1) * P, :]
             nc.scalar.copy(out=o[:, 0:512], in_=big[:])
             nc.vector.tensor_copy(out=o[:, 512:E], in_=small[:, 0:256])
-            rows = out[block * P : (block + 1) * P, :]
-            if last:
+            if block == T // P - 1:
                 nc.sync.dma_start(out=rows[:, 0:512], in_=o[:, 0:512])
                 nc.sync.dma_start(out=rows[:, 512:E], in_=o[:, 512:E])
+            elif block >= 16:
+                nc.sync.dma_start(out=rows, in_=o[:])
             else:
                 nc.gpsimd.dma_start(out=rows, in_=o[:])
 
@@ -105,7 +114,7 @@ def tile_longcatrouter_kernel(tc, x_words, x_scales, w_words, w_scales, out):
                 mm(accs[j][0], 0, j, g, 0, 512)
                 mm(accs[j][1], 0, j, g, 512, E)
         for j in range(NB):
-            finish(accs[j][0], accs[j][1], j, False)
+            finish(accs[j][0], accs[j][1], j)
 
         for block in range(NB, T // P):
             c, j = block // NB, block % NB
@@ -114,4 +123,4 @@ def tile_longcatrouter_kernel(tc, x_words, x_scales, w_words, w_scales, out):
                 mm(big, c, j, g, 0, 512)
             for g in range(PASSES):
                 mm(small, c, j, g, 512, E)
-            finish(big, small, block, block == T // P - 1)
+            finish(big, small, block)

@@ -16,8 +16,9 @@ PASSES = D // 512
 CHUNK = 512
 NB = CHUNK // P
 NC = T // CHUNK
-WARM = 32
-RUNS = ((0, 3), (3, 8))
+WARM = 40
+W_RUNS = ((0, 4), (4, 8))
+X_RUNS = ((0, 2), (2, 8))
 
 
 def tile_longcatrouter_kernel(tc, x_words, x_scales, w_words, w_scales, out):
@@ -45,35 +46,39 @@ def tile_longcatrouter_kernel(tc, x_words, x_scales, w_words, w_scales, out):
                 )
 
         warm = keep.tile([P, P], BF16, name="warm")
-        nc.vector.memset(warm[:], 0.0)
+        nc.gpsimd.memset(warm[:], 0.0)
 
         wc = [alloc("wc%d" % g, 1, 2 * E) for g in range(PASSES)]
         xc0 = [alloc("xc0_%d" % g, 1, 2 * CHUNK) for g in range(PASSES)]
-        wp = [alloc("wp%d" % a, b - a, E) for a, b in RUNS]
-        xp0 = [alloc("xp0_%d" % a, b - a, CHUNK) for a, b in RUNS]
+        wp = [alloc("wp%d" % a, b - a, E) for a, b in W_RUNS]
+        xp0 = [alloc("xp0_%d" % a, b - a, CHUNK) for a, b in X_RUNS]
         xc = [None] + [alloc("xc%d" % c, PASSES, 2 * CHUNK) for c in range(1, NC)]
         xp = [None] + [alloc("xp%d" % c, PASSES, CHUNK) for c in range(1, NC)]
-        for i in range(len(RUNS)):
-            zero(wp[i])
-            zero(xp0[i])
+        for t in (wp[0], xp0[0], xp0[1], wp[1]):
+            zero(t)
         for c in range(1, NC):
             zero(xp[c])
 
-        for i, (a, b) in enumerate(RUNS):
-            for g in range(a, b):
+        for g in range(PASSES):
+            if g == 0:
                 load_codes(xc0[g], x_words, g, g + 1, 0, 2 * CHUNK)
                 load_codes(wc[g], w_words, g, g + 1, 0, 2 * E)
+            for i, (a, b) in enumerate(W_RUNS):
                 if g == a:
                     load_scales(wp[i], w_scales, a, b, 0, E)
+            for i, (a, b) in enumerate(X_RUNS):
+                if g == a:
                     load_scales(xp0[i], x_scales, a, b, 0, CHUNK)
+            if g > 0:
+                load_codes(xc0[g], x_words, g, g + 1, 0, 2 * CHUNK)
+                load_codes(wc[g], w_words, g, g + 1, 0, 2 * E)
         for c in range(1, NC):
             load_codes(xc[c], x_words, 0, PASSES, 2 * c * CHUNK, 2 * (c + 1) * CHUNK)
             load_scales(xp[c], x_scales, 0, PASSES, c * CHUNK, (c + 1) * CHUNK)
 
-        def run_of(g):
-            for i, (a, b) in enumerate(RUNS):
-                if g < b:
-                    return i, g - a
+        def run_of(runs, g):
+            i = 0 if g < runs[0][1] else 1
+            return i, g - runs[i][0]
 
         def bank(k):
             return psum.tile([P, 512], F32, tag="bank%d" % k, name="bank%d" % k)
@@ -83,8 +88,9 @@ def tile_longcatrouter_kernel(tc, x_words, x_scales, w_words, w_scales, out):
             nc.tensor.matmul(dummy[:, 0:P], warm[:], warm[:], start=True, stop=True)
 
         def mm(acc, c, j, g, n0, n1):
-            i, k = run_of(g)
-            xct, xci, xpt, xpi = (xc0[g], 0, xp0[i], k) if c == 0 else (xc[c], g, xp[c], g)
+            i, k = run_of(W_RUNS, g)
+            xi, xk = run_of(X_RUNS, g)
+            xct, xci, xpt, xpi = (xc0[g], 0, xp0[xi], xk) if c == 0 else (xc[c], g, xp[c], g)
             nc.tensor.matmul_mx(
                 out=acc[:, 0 : n1 - n0],
                 lhsT=xct[:, xci, 256 * j : 256 * (j + 1)].bitcast(F4),
@@ -119,8 +125,13 @@ def tile_longcatrouter_kernel(tc, x_words, x_scales, w_words, w_scales, out):
         for block in range(NB, T // P):
             c, j = block // NB, block % NB
             big, small = bank(2 * j), bank(2 * j + 1)
-            for g in range(PASSES):
-                mm(big, c, j, g, 0, 512)
-            for g in range(PASSES):
-                mm(small, c, j, g, 512, E)
+            if block == T // P - 1:
+                for g in range(PASSES):
+                    mm(big, c, j, g, 0, 512)
+                for g in range(PASSES):
+                    mm(small, c, j, g, 512, E)
+            else:
+                for g in range(PASSES):
+                    mm(big, c, j, g, 0, 512)
+                    mm(small, c, j, g, 512, E)
             finish(big, small, block)

@@ -9,129 +9,142 @@ F32 = mybir.dt.float32
 BF16 = mybir.dt.bfloat16
 I32 = mybir.dt.int32
 U8 = mybir.dt.uint8
-F4 = mybir.dt.float4_e2m1fn_x4
+FP4X4 = mybir.dt.float4_e2m1fn_x4
 
 P = 128
 PASSES = D // 512
-CHUNK = 512
-NB = CHUNK // P
-NC = T // CHUNK
-WARM = 40
+BIG = 512
+SMALL = E - BIG
+WORD = 2
+
+PIECES = ((0, 512), (512, 1024), (1024, 2048), (2048, 4096))
+FIRST_BLOCKS = PIECES[0][1] // P
+
 W_RUNS = ((0, 4), (4, 8))
-X_RUNS = ((0, 2), (2, 8))
+X_RUNS = ((0, 3), (3, 8))
+EACH = tuple((g, g + 1) for g in range(PASSES))
+ALL = ((0, PASSES),)
+
+WARM_UPS = 36
 
 
 def tile_longcatrouter_kernel(tc, x_words, x_scales, w_words, w_scales, out):
     nc = tc.nc
     with ExitStack() as ctx:
         keep = ctx.enter_context(tc.tile_pool(name="keep", bufs=1))
-        res = ctx.enter_context(tc.tile_pool(name="res", bufs=8))
+        results = ctx.enter_context(tc.tile_pool(name="results", bufs=16))
         psum = ctx.enter_context(tc.psum_pool(name="psum", bufs=1))
         ctx.enter_context(tc.manual_schedule())
 
-        def alloc(name, passes, width):
-            return keep.tile([P, passes, width], U8, align_bytes=256, name=name)
+        def tiles(name, runs, width):
+            return [keep.tile([P, b - a, width], U8, align_bytes=256, name="%s_%d" % (name, a)) for a, b in runs]
 
-        def zero(t):
-            nc.vector.memset(t[:].bitcast(I32), 0)
+        def of_pass(run_tiles, runs, g):
+            i = [a <= g < b for a, b in runs].index(True)
+            return run_tiles[i], g - runs[i][0]
 
-        def load_codes(t, words, a, b, c0, c1):
-            nc.sync.dma_start(out=t[:].bitcast(I32), in_=words[a:b, :, c0:c1].rearrange("g p n -> p g n").bitcast(I32))
-
-        def load_scales(t, scales, a, b, c0, c1):
-            for r in range(4):
-                nc.sync.dma_start(
-                    out=t[r:P:32, :, :].bitcast(I32),
-                    in_=scales[a:b, r:16:4, c0:c1].rearrange("g q n -> q g n").bitcast(I32),
-                )
+        w_codes = tiles("w_codes", EACH, WORD * E)
+        w_planes = tiles("w_planes", W_RUNS, E)
+        x_code_runs = [EACH] + [ALL] * (len(PIECES) - 1)
+        x_plane_runs = [X_RUNS] + [ALL] * (len(PIECES) - 1)
+        x_codes = [tiles("x_codes%d" % i, x_code_runs[i], WORD * (t1 - t0)) for i, (t0, t1) in enumerate(PIECES)]
+        x_planes = [tiles("x_planes%d" % i, x_plane_runs[i], t1 - t0) for i, (t0, t1) in enumerate(PIECES)]
 
         warm = keep.tile([P, P], BF16, name="warm")
         nc.gpsimd.memset(warm[:], 0.0)
 
-        wc = [alloc("wc%d" % g, 1, 2 * E) for g in range(PASSES)]
-        xc0 = [alloc("xc0_%d" % g, 1, 2 * CHUNK) for g in range(PASSES)]
-        wp = [alloc("wp%d" % a, b - a, E) for a, b in W_RUNS]
-        xp0 = [alloc("xp0_%d" % a, b - a, CHUNK) for a, b in X_RUNS]
-        xc = [None] + [alloc("xc%d" % c, PASSES, 2 * CHUNK) for c in range(1, NC)]
-        xp = [None] + [alloc("xp%d" % c, PASSES, CHUNK) for c in range(1, NC)]
-        for t in (wp[0], xp0[0], xp0[1], wp[1]):
-            zero(t)
-        for c in range(1, NC):
-            zero(xp[c])
+        def zero(plane):
+            nc.vector.memset(plane[:].bitcast(I32), 0)
 
+        for plane in (w_planes[0], x_planes[0][0], x_planes[0][1], w_planes[1]):
+            zero(plane)
+        for i in range(1, len(PIECES)):
+            zero(x_planes[i][0])
+
+        def load_codes(tile, words, a, b, c0, c1):
+            src = words[a:b, :, WORD * c0 : WORD * c1].rearrange("g p n -> p g n")
+            nc.sync.dma_start(out=tile[:].bitcast(I32), in_=src.bitcast(I32))
+
+        def load_scales(plane, scales, a, b, c0, c1):
+            for r in range(4):
+                src = scales[a:b, r:16:4, c0:c1].rearrange("g q n -> q g n")
+                nc.sync.dma_start(out=plane[r:P:32, :, :].bitcast(I32), in_=src.bitcast(I32))
+
+        def load_piece(i):
+            t0, t1 = PIECES[i]
+            load_codes(x_codes[i][0], x_words, 0, PASSES, t0, t1)
+            load_scales(x_planes[i][0], x_scales, 0, PASSES, t0, t1)
+
+        def load_codes_of_pass(g):
+            load_codes(x_codes[0][g], x_words, g, g + 1, *PIECES[0])
+            load_codes(w_codes[g], w_words, g, g + 1, 0, E)
+
+        load_codes_of_pass(0)
         for g in range(PASSES):
-            if g == 0:
-                load_codes(xc0[g], x_words, g, g + 1, 0, 2 * CHUNK)
-                load_codes(wc[g], w_words, g, g + 1, 0, 2 * E)
-            for i, (a, b) in enumerate(W_RUNS):
-                if g == a:
-                    load_scales(wp[i], w_scales, a, b, 0, E)
-            for i, (a, b) in enumerate(X_RUNS):
-                if g == a:
-                    load_scales(xp0[i], x_scales, a, b, 0, CHUNK)
+            for plane, (a, b) in zip(w_planes, W_RUNS):
+                if a == g:
+                    load_scales(plane, w_scales, a, b, 0, E)
+            for plane, (a, b) in zip(x_planes[0], X_RUNS):
+                if a == g:
+                    load_scales(plane, x_scales, a, b, *PIECES[0])
             if g > 0:
-                load_codes(xc0[g], x_words, g, g + 1, 0, 2 * CHUNK)
-                load_codes(wc[g], w_words, g, g + 1, 0, 2 * E)
-        for c in range(1, NC):
-            load_codes(xc[c], x_words, 0, PASSES, 2 * c * CHUNK, 2 * (c + 1) * CHUNK)
-            load_scales(xp[c], x_scales, 0, PASSES, c * CHUNK, (c + 1) * CHUNK)
+                load_codes_of_pass(g)
+        load_piece(1)
+        load_piece(2)
 
-        def run_of(runs, g):
-            i = 0 if g < runs[0][1] else 1
-            return i, g - runs[i][0]
+        def bank(i):
+            return psum.tile([P, BIG], F32, tag="bank%d" % i, name="bank%d" % i)
 
-        def bank(k):
-            return psum.tile([P, 512], F32, tag="bank%d" % k, name="bank%d" % k)
+        warm_bank = bank(7)
+        for i in range(WARM_UPS):
+            nc.tensor.matmul(warm_bank[:, 0:P], warm[:], warm[:], start=True, stop=True)
 
-        dummy = bank(7)
-        for i in range(WARM):
-            nc.tensor.matmul(dummy[:, 0:P], warm[:], warm[:], start=True, stop=True)
-
-        def mm(acc, c, j, g, n0, n1):
-            i, k = run_of(W_RUNS, g)
-            xi, xk = run_of(X_RUNS, g)
-            xct, xci, xpt, xpi = (xc0[g], 0, xp0[xi], xk) if c == 0 else (xc[c], g, xp[c], g)
+        def multiply(acc, block, g, e0, e1):
+            tok = P * block
+            i = [t0 <= tok < t1 for t0, t1 in PIECES].index(True)
+            col = tok - PIECES[i][0]
+            xc, xc_g = of_pass(x_codes[i], x_code_runs[i], g)
+            xp, xp_g = of_pass(x_planes[i], x_plane_runs[i], g)
+            wp, wp_g = of_pass(w_planes, W_RUNS, g)
             nc.tensor.matmul_mx(
-                out=acc[:, 0 : n1 - n0],
-                lhsT=xct[:, xci, 256 * j : 256 * (j + 1)].bitcast(F4),
-                lhsT_scale=xpt[:, xpi, P * j : P * (j + 1)],
-                rhs=wc[g][:, 0, 2 * n0 : 2 * n1].bitcast(F4),
-                rhs_scale=wp[i][:, k, n0:n1],
+                out=acc[:, 0 : e1 - e0],
+                lhsT=xc[:, xc_g, WORD * col : WORD * (col + P)].bitcast(FP4X4),
+                lhsT_scale=xp[:, xp_g, col : col + P],
+                rhs=w_codes[g][:, 0, WORD * e0 : WORD * e1].bitcast(FP4X4),
+                rhs_scale=wp[:, wp_g, e0:e1],
                 start=(g == 0),
                 stop=(g == PASSES - 1),
             )
 
-        def finish(big, small, block):
-            o = res.tile([P, E], F32, name="o")
-            rows = out[block * P : (block + 1) * P, :]
-            nc.scalar.copy(out=o[:, 0:512], in_=big[:])
-            nc.vector.tensor_copy(out=o[:, 512:E], in_=small[:, 0:256])
-            if block == T // P - 1:
-                nc.sync.dma_start(out=rows[:, 0:512], in_=o[:, 0:512])
-                nc.sync.dma_start(out=rows[:, 512:E], in_=o[:, 512:E])
-            elif block >= 16:
-                nc.sync.dma_start(out=rows, in_=o[:])
-            else:
-                nc.gpsimd.dma_start(out=rows, in_=o[:])
+        last = T // P - 1
 
-        accs = [(bank(2 * j), bank(2 * j + 1)) for j in range(NB)]
+        def store(big, small, block):
+            logits = results.tile([P, E], F32, name="logits")
+            rows = out[P * block : P * (block + 1), :]
+            nc.scalar.copy(out=logits[:, 0:BIG], in_=big[:])
+            nc.vector.tensor_copy(out=logits[:, BIG:E], in_=small[:, 0:SMALL])
+            if block < last:
+                nc.sync.dma_start(out=rows, in_=logits[:])
+            else:
+                nc.sync.dma_start(out=rows[:, 0:BIG], in_=logits[:, 0:BIG])
+                nc.sync.dma_start(out=rows[:, BIG:E], in_=logits[:, BIG:E])
+
+        banks = [(bank(2 * block), bank(2 * block + 1)) for block in range(FIRST_BLOCKS)]
         for g in range(PASSES):
-            for j in range(NB):
-                mm(accs[j][0], 0, j, g, 0, 512)
-                mm(accs[j][1], 0, j, g, 512, E)
-        for j in range(NB):
-            finish(accs[j][0], accs[j][1], j)
+            for block in range(FIRST_BLOCKS):
+                big, small = banks[block]
+                multiply(big, block, g, 0, BIG)
+                multiply(small, block, g, BIG, E)
+        for block in range(FIRST_BLOCKS):
+            store(*banks[block], block)
 
-        for block in range(NB, T // P):
-            c, j = block // NB, block % NB
+        load_piece(3)
+
+        for block in range(FIRST_BLOCKS, last + 1):
+            j = block % FIRST_BLOCKS
             big, small = bank(2 * j), bank(2 * j + 1)
-            if block == T // P - 1:
-                for g in range(PASSES):
-                    mm(big, c, j, g, 0, 512)
-                for g in range(PASSES):
-                    mm(small, c, j, g, 512, E)
-            else:
-                for g in range(PASSES):
-                    mm(big, c, j, g, 0, 512)
-                    mm(small, c, j, g, 512, E)
-            finish(big, small, block)
+            for g in range(PASSES):
+                multiply(big, block, g, 0, BIG)
+            for g in range(PASSES):
+                multiply(small, block, g, BIG, E)
+            store(big, small, block)

from contextlib import ExitStack

import concourse.mybir as mybir

T, D, E = 4096, 4096, 768
FLOPS = 2 * T * D * E

F32 = mybir.dt.float32
BF16 = mybir.dt.bfloat16
I32 = mybir.dt.int32
U8 = mybir.dt.uint8
FP4X4 = mybir.dt.float4_e2m1fn_x4

P = 128
PASSES = D // 512
BIG = 512
SMALL = E - BIG
WORD = 2

PIECES = ((0, 512), (512, 1024), (1024, 2048), (2048, 4096))
FIRST_BLOCKS = PIECES[0][1] // P

W_RUNS = ((0, 4), (4, 8))
X_RUNS = ((0, 3), (3, 8))
EACH = tuple((g, g + 1) for g in range(PASSES))
ALL = ((0, PASSES),)

WARM_UPS = 36


def tile_longcatrouter_kernel(tc, x_words, x_scales, w_words, w_scales, out):
    nc = tc.nc
    with ExitStack() as ctx:
        keep = ctx.enter_context(tc.tile_pool(name="keep", bufs=1))
        results = ctx.enter_context(tc.tile_pool(name="results", bufs=16))
        psum = ctx.enter_context(tc.psum_pool(name="psum", bufs=1))
        ctx.enter_context(tc.manual_schedule())

        def tiles(name, runs, width):
            return [keep.tile([P, b - a, width], U8, align_bytes=256, name="%s_%d" % (name, a)) for a, b in runs]

        def of_pass(run_tiles, runs, g):
            i = [a <= g < b for a, b in runs].index(True)
            return run_tiles[i], g - runs[i][0]

        w_codes = tiles("w_codes", EACH, WORD * E)
        w_planes = tiles("w_planes", W_RUNS, E)
        x_code_runs = [EACH] + [ALL] * (len(PIECES) - 1)
        x_plane_runs = [X_RUNS] + [ALL] * (len(PIECES) - 1)
        x_codes = [tiles("x_codes%d" % i, x_code_runs[i], WORD * (t1 - t0)) for i, (t0, t1) in enumerate(PIECES)]
        x_planes = [tiles("x_planes%d" % i, x_plane_runs[i], t1 - t0) for i, (t0, t1) in enumerate(PIECES)]

        warm = keep.tile([P, P], BF16, name="warm")
        nc.gpsimd.memset(warm[:], 0.0)

        def zero(plane):
            nc.vector.memset(plane[:].bitcast(I32), 0)

        for plane in (w_planes[0], x_planes[0][0], x_planes[0][1], w_planes[1]):
            zero(plane)
        for i in range(1, len(PIECES)):
            zero(x_planes[i][0])

        def load_codes(tile, words, a, b, c0, c1):
            src = words[a:b, :, WORD * c0 : WORD * c1].rearrange("g p n -> p g n")
            nc.sync.dma_start(out=tile[:].bitcast(I32), in_=src.bitcast(I32))

        def load_scales(plane, scales, a, b, c0, c1):
            for r in range(4):
                src = scales[a:b, r:16:4, c0:c1].rearrange("g q n -> q g n")
                nc.sync.dma_start(out=plane[r:P:32, :, :].bitcast(I32), in_=src.bitcast(I32))

        def load_piece(i):
            t0, t1 = PIECES[i]
            load_codes(x_codes[i][0], x_words, 0, PASSES, t0, t1)
            load_scales(x_planes[i][0], x_scales, 0, PASSES, t0, t1)

        def load_codes_of_pass(g):
            load_codes(x_codes[0][g], x_words, g, g + 1, *PIECES[0])
            load_codes(w_codes[g], w_words, g, g + 1, 0, E)

        load_codes_of_pass(0)
        for g in range(PASSES):
            for plane, (a, b) in zip(w_planes, W_RUNS):
                if a == g:
                    load_scales(plane, w_scales, a, b, 0, E)
            for plane, (a, b) in zip(x_planes[0], X_RUNS):
                if a == g:
                    load_scales(plane, x_scales, a, b, *PIECES[0])
            if g > 0:
                load_codes_of_pass(g)
        load_piece(1)
        load_piece(2)

        def bank(i):
            return psum.tile([P, BIG], F32, tag="bank%d" % i, name="bank%d" % i)

        warm_bank = bank(7)
        for i in range(WARM_UPS):
            nc.tensor.matmul(warm_bank[:, 0:P], warm[:], warm[:], start=True, stop=True)

        def multiply(acc, block, g, e0, e1):
            tok = P * block
            i = [t0 <= tok < t1 for t0, t1 in PIECES].index(True)
            col = tok - PIECES[i][0]
            xc, xc_g = of_pass(x_codes[i], x_code_runs[i], g)
            xp, xp_g = of_pass(x_planes[i], x_plane_runs[i], g)
            wp, wp_g = of_pass(w_planes, W_RUNS, g)
            nc.tensor.matmul_mx(
                out=acc[:, 0 : e1 - e0],
                lhsT=xc[:, xc_g, WORD * col : WORD * (col + P)].bitcast(FP4X4),
                lhsT_scale=xp[:, xp_g, col : col + P],
                rhs=w_codes[g][:, 0, WORD * e0 : WORD * e1].bitcast(FP4X4),
                rhs_scale=wp[:, wp_g, e0:e1],
                start=(g == 0),
                stop=(g == PASSES - 1),
            )

        last = T // P - 1

        def store(big, small, block):
            logits = results.tile([P, E], F32, name="logits")
            rows = out[P * block : P * (block + 1), :]
            nc.scalar.copy(out=logits[:, 0:BIG], in_=big[:])
            nc.vector.tensor_copy(out=logits[:, BIG:E], in_=small[:, 0:SMALL])
            if block < last:
                nc.sync.dma_start(out=rows, in_=logits[:])
            else:
                nc.sync.dma_start(out=rows[:, 0:BIG], in_=logits[:, 0:BIG])
                nc.sync.dma_start(out=rows[:, BIG:E], in_=logits[:, BIG:E])

        banks = [(bank(2 * block), bank(2 * block + 1)) for block in range(FIRST_BLOCKS)]
        for g in range(PASSES):
            for block in range(FIRST_BLOCKS):
                big, small = banks[block]
                multiply(big, block, g, 0, BIG)
                multiply(small, block, g, BIG, E)
        for block in range(FIRST_BLOCKS):
            store(*banks[block], block)

        load_piece(3)

        for block in range(FIRST_BLOCKS, last + 1):
            j = block % FIRST_BLOCKS
            big, small = bank(2 * j), bank(2 * j + 1)
            for g in range(PASSES):
                multiply(big, block, g, 0, BIG)
            for g in range(PASSES):
                multiply(small, block, g, BIG, E)
            store(big, small, block)
